import numpy as np
import ml_dtypes


def mxq(x, axis, fmt="e4m3"):
    dtype, down = {"e4m3": (ml_dtypes.float8_e4m3fn, 7), "e5m2": (ml_dtypes.float8_e5m2, 14)}[fmt]
    v = np.moveaxis(np.asarray(x, np.float32).astype(ml_dtypes.bfloat16).astype(np.float64), axis, -1)
    blocks = v.reshape(v.shape[:-1] + (-1, 32))
    amax = np.abs(blocks).max(-1, keepdims=True)
    byte = np.maximum(np.where(amax > 0, np.frexp(amax)[1] - 1 + 127, 0) - down, 1)
    scale = np.exp2(byte - 127.0)
    codes = (blocks / scale).astype(np.float32).astype(dtype).astype(np.float64)
    return np.moveaxis((codes * scale).reshape(v.shape), -1, axis)


WIDE = False


def mx_kscale(k):
    if not WIDE:
        return np.ones(k)
    levels = np.array([20, -20, 10, -10, 0])
    a = np.random.permutation(np.resize(levels, k // 512 * 4)).reshape(k // 512, 4)
    idx = np.arange(k)
    return np.exp2(a[idx // 512, idx % 128 // 32])


BF16 = ml_dtypes.bfloat16


def bf(x):
    return np.asarray(x, np.float32).astype(BF16)


def f64(x):
    return np.asarray(x).astype(np.float64)


B, S, D_IN, D_OUT = 4, 2048, 512, 512
T = B * S
X_STEP = 2.0 ** -5
W_STEP = 2.0 ** -9
B_STEP = 2.0 ** -6


def on_grid(a, step):
    q = np.clip(np.round(a / step), -127, 127)
    q.flat[0] = 127.0
    return q * step


def setup_inputs():
    s = mx_kscale(T).reshape(B, S, 1)
    x = on_grid(np.random.standard_normal((B, S, D_IN)), X_STEP) * s
    W = on_grid(np.random.standard_normal((D_OUT, D_IN)) / np.sqrt(D_IN), W_STEP)
    b = np.round(np.random.standard_normal(D_OUT) * 0.3 / B_STEP) * B_STEP
    g = np.random.standard_normal((B, S, D_OUT)) * np.exp2(np.random.randint(-12, 1, (B, S, 1))) * 0.25 / s
    return {"x": bf(x), "W": bf(W), "b": bf(b), "grad_out": bf(g)}


def reference(x, W, b, grad_out):
    xt = f64(x).reshape(T, D_IN)
    gt = f64(grad_out).reshape(T, D_OUT)
    return mxq(gt, 0, "e5m2").T @ mxq(xt, 0, "e4m3")

@@ -1,0 +1,96 @@
+from contextlib import ExitStack
+
+import concourse.mybir as mybir
+
+F32 = mybir.dt.float32
+BF16 = mybir.dt.bfloat16
+U32 = mybir.dt.uint32
+U8 = mybir.dt.uint8
+E4M3X4 = mybir.dt.float8_e4m3fn_x4
+E5M2X4 = mybir.dt.float8_e5m2_x4
+
+P = 128
+PACK = 4
+K_PASS = P * PACK
+TOKENS = 8192
+D_IN = 512
+D_OUT = 512
+PASSES = TOKENS // K_PASS
+M_TILES = D_OUT // P
+
+FLOPS = 2 * TOKENS * D_IN * D_OUT
+BYTES = 2 * TOKENS * (D_IN + D_OUT) + 4 * D_IN * D_OUT
+
+
+def regroup(engine_copy, grouped, raw):
+    engine_copy(
+        out=grouped.rearrange("p (c i) t -> p c t i", i=4),
+        in_=raw.rearrange("p t (c i) -> p c t i", i=4),
+    )
+
+
+def tile_quantlinearwrapper_t_kernel(tc, x, W, b, grad_out, out):
+    nc = tc.nc
+    x_rows = x.flatten_outer_dims()
+    g_rows = grad_out.flatten_outer_dims()
+
+    with ExitStack() as ctx:
+        ctx.enter_context(tc.manual_schedule())
+        raw_pool = ctx.enter_context(tc.tile_pool(name="raw", bufs=PASSES))
+        grp_pool = ctx.enter_context(tc.tile_pool(name="grp", bufs=3))
+        code_pool = ctx.enter_context(tc.tile_pool(name="code", bufs=3))
+        res_pool = ctx.enter_context(tc.tile_pool(name="res", bufs=M_TILES))
+        psum = ctx.enter_context(tc.psum_pool(name="acc", bufs=1))
+
+        g_raw = []
+        x_raw = []
+        for c in range(PASSES):
+            rows = slice(c * K_PASS, (c + 1) * K_PASS)
+            g_in = raw_pool.tile([P, PACK, D_OUT], BF16, tag="g_raw", name="g_in")
+            nc.sync.dma_start(out=g_in[:], in_=g_rows[rows, :].rearrange("(p j) w -> p j w", j=PACK))
+            g_raw.append(g_in)
+            x_in = raw_pool.tile([P, PACK, D_IN], BF16, tag="x_raw", name="x_in")
+            nc.sync.dma_start(out=x_in[:], in_=x_rows[rows, :].rearrange("(p j) w -> p j w", j=PACK))
+            x_raw.append(x_in)
+
+        acc = [psum.tile([P, D_IN], F32, tag="acc%d" % m, name="acc%d" % m) for m in range(M_TILES)]
+
+        for c in range(PASSES):
+            g_grp = grp_pool.tile([P, D_OUT, PACK], BF16, tag="g_grp", align_bytes=64)
+            x_grp = grp_pool.tile([P, D_IN, PACK], BF16, tag="x_grp", align_bytes=64)
+            regroup(nc.scalar.copy, g_grp[:], g_raw[c][:])
+            regroup(nc.vector.tensor_copy, x_grp[:], x_raw[c][:])
+
+            g_codes = code_pool.tile([P, D_OUT], U32, tag="g_codes", align_bytes=64)
+            g_scales = code_pool.tile([P, D_OUT], U8, tag="g_scales", align_bytes=64)
+            x_codes = code_pool.tile([P, D_IN], U32, tag="x_codes", align_bytes=64)
+            x_scales = code_pool.tile([P, D_IN], U8, tag="x_scales", align_bytes=64)
+            nc.vector.quantize_mx(
+                out=g_codes[:].bitcast(E5M2X4),
+                scales=g_scales[:],
+                in_=g_grp[:].rearrange("p w j -> p (w j)"),
+            )
+            nc.vector.quantize_mx(
+                out=x_codes[:].bitcast(E4M3X4),
+                scales=x_scales[:],
+                in_=x_grp[:].rearrange("p w j -> p (w j)"),
+            )
+            for m in range(M_TILES):
+                cols = slice(m * P, (m + 1) * P)
+                nc.tensor.matmul_mx(
+                    out=acc[m][:],
+                    lhsT=g_codes[:, cols].bitcast(E5M2X4),
+                    lhsT_scale=g_scales[:, cols],
+                    rhs=x_codes[:].bitcast(E4M3X4),
+                    rhs_scale=x_scales[:],
+                    start=(c == 0),
+                    stop=(c == PASSES - 1),
+                )
+
+        for m in range(M_TILES):
+            res = res_pool.tile([P, D_IN], F32, tag="res")
+            if m % 2 == 0:
+                nc.vector.tensor_copy(out=res[:], in_=acc[m][:])
+            else:
+                nc.scalar.copy(out=res[:], in_=acc[m][:])
+            nc.sync.dma_start(out=out[m * P : (m + 1) * P, :], in_=res[:])

@@ -1,6 +1,7 @@
 from contextlib import ExitStack
 
 import concourse.mybir as mybir
+from concourse.masks import make_identity
 
 F32 = mybir.dt.float32
 BF16 = mybir.dt.bfloat16
@@ -16,16 +17,22 @@ TOKENS = 8192
 D_IN = 512
 D_OUT = 512
 PASSES = TOKENS // K_PASS
+LAST = PASSES - 1
 M_TILES = D_OUT // P
+HALF = 256
+
+TENSOR_PASSES = range(7, 15)
+S_X_COLS = 112
+LAST_S_X_COLS = 320
 
 FLOPS = 2 * TOKENS * D_IN * D_OUT
 BYTES = 2 * TOKENS * (D_IN + D_OUT) + 4 * D_IN * D_OUT
 
 
-def regroup(engine_copy, grouped, raw):
+def regroup(engine_copy, grouped, raw, lo, hi):
     engine_copy(
-        out=grouped.rearrange("p (c i) t -> p c t i", i=4),
-        in_=raw.rearrange("p t (c i) -> p c t i", i=4),
+        out=grouped[:, lo:hi, :].rearrange("p (c i) t -> p c t i", i=4),
+        in_=raw[:, :, lo:hi].rearrange("p t (c i) -> p c t i", i=4),
     )
 
 
@@ -36,61 +43,120 @@ def tile_quantlinearwrapper_t_kernel(tc, x, W, b, grad_out, out):
 
     with ExitStack() as ctx:
         ctx.enter_context(tc.manual_schedule())
+        const_pool = ctx.enter_context(tc.tile_pool(name="const", bufs=1))
         raw_pool = ctx.enter_context(tc.tile_pool(name="raw", bufs=PASSES))
         grp_pool = ctx.enter_context(tc.tile_pool(name="grp", bufs=3))
         code_pool = ctx.enter_context(tc.tile_pool(name="code", bufs=3))
         res_pool = ctx.enter_context(tc.tile_pool(name="res", bufs=M_TILES))
         psum = ctx.enter_context(tc.psum_pool(name="acc", bufs=1))
+        mv_psum = ctx.enter_context(tc.psum_pool(name="mv", bufs=2))
 
-        g_raw = []
-        x_raw = []
-        for c in range(PASSES):
+        g_raw = {}
+        x_raw = {}
+
+        def load(store, rows_ap, c, tag):
             rows = slice(c * K_PASS, (c + 1) * K_PASS)
-            g_in = raw_pool.tile([P, PACK, D_OUT], BF16, tag="g_raw", name="g_in")
-            nc.sync.dma_start(out=g_in[:], in_=g_rows[rows, :].rearrange("(p j) w -> p j w", j=PACK))
-            g_raw.append(g_in)
-            x_in = raw_pool.tile([P, PACK, D_IN], BF16, tag="x_raw", name="x_in")
-            nc.sync.dma_start(out=x_in[:], in_=x_rows[rows, :].rearrange("(p j) w -> p j w", j=PACK))
-            x_raw.append(x_in)
+            raw = raw_pool.tile([P, PACK, D_IN], BF16, tag=tag, name=tag)
+            nc.sync.dma_start(out=raw[:], in_=rows_ap[rows, :].rearrange("(p j) w -> p j w", j=PACK))
+            store[c] = raw
+
+        for c in range(LAST):
+            load(g_raw, g_rows, c, "g_raw")
+            load(x_raw, x_rows, c, "x_raw")
+        load(x_raw, x_rows, LAST, "x_raw")
+        load(g_raw, g_rows, LAST, "g_raw")
+
+        ident = const_pool.tile([P, P], BF16)
+        make_identity(nc, ident[:])
 
         acc = [psum.tile([P, D_IN], F32, tag="acc%d" % m, name="acc%d" % m) for m in range(M_TILES)]
 
+        def tensor_part(c):
+            if c not in TENSOR_PASSES:
+                return None
+            bank = mv_psum.tile([P, HALF, PACK], BF16, tag="bank", name="bank")
+            for j in (1, 0, 3, 2):
+                cols = g_raw[c][:, j, 0:HALF]
+                if j % 2 == 1:
+                    nc.tensor.matmul(
+                        out=bank[:, :, j - 1 : j + 1],
+                        lhsT=ident[:],
+                        rhs=cols.unsqueeze(2).to_broadcast([P, HALF, 2]),
+                        start=True,
+                        stop=True,
+                    )
+                else:
+                    nc.tensor.matmul(out=bank[:, :, j], lhsT=ident[:], rhs=cols, start=True, stop=True)
+            return bank
+
+        def new_tiles():
+            g_grp = grp_pool.tile([P, D_OUT, PACK], BF16, tag="g_grp", align_bytes=64, name="g_grp")
+            x_grp = grp_pool.tile([P, D_IN, PACK], BF16, tag="x_grp", align_bytes=64, name="x_grp")
+            return g_grp, x_grp
+
+        def copies(c, bank):
+            g_grp, x_grp = new_tiles()
+            if bank is None:
+                regroup(nc.scalar.copy, g_grp, g_raw[c], 0, D_OUT)
+                regroup(nc.vector.tensor_copy, x_grp, x_raw[c], 0, D_IN)
+            else:
+                regroup(nc.scalar.copy, g_grp, g_raw[c], HALF, D_OUT)
+                nc.scalar.copy(out=g_grp[:, 0:HALF, :], in_=bank[:])
+                regroup(nc.scalar.copy, x_grp, x_raw[c], 0, S_X_COLS)
+                regroup(nc.vector.tensor_copy, x_grp, x_raw[c], S_X_COLS, D_IN)
+            return g_grp, x_grp
+
+        def last_copies():
+            g_grp, x_grp = new_tiles()
+            regroup(nc.scalar.copy, x_grp, x_raw[LAST], 0, LAST_S_X_COLS)
+            regroup(nc.vector.tensor_copy, x_grp, x_raw[LAST], LAST_S_X_COLS, D_IN)
+            regroup(nc.vector.tensor_copy, g_grp, g_raw[LAST], 0, P)
+            for m in range(1, M_TILES):
+                regroup(nc.scalar.copy, g_grp, g_raw[LAST], m * P, (m + 1) * P)
+            return g_grp, x_grp
+
+        def quantise(codes, scales, grouped, lo, hi, fmt):
+            nc.vector.quantize_mx(
+                out=codes[:, lo:hi].bitcast(fmt),
+                scales=scales[:, lo:hi],
+                in_=grouped[:, lo:hi, :].rearrange("p w j -> p (w j)"),
+            )
+
+        grouped = copies(0, tensor_part(0))
         for c in range(PASSES):
-            g_grp = grp_pool.tile([P, D_OUT, PACK], BF16, tag="g_grp", align_bytes=64)
-            x_grp = grp_pool.tile([P, D_IN, PACK], BF16, tag="x_grp", align_bytes=64)
-            regroup(nc.scalar.copy, g_grp[:], g_raw[c][:])
-            regroup(nc.vector.tensor_copy, x_grp[:], x_raw[c][:])
+            g_grp, x_grp = grouped
+            bank = tensor_part(c + 1)
 
             g_codes = code_pool.tile([P, D_OUT], U32, tag="g_codes", align_bytes=64)
             g_scales = code_pool.tile([P, D_OUT], U8, tag="g_scales", align_bytes=64)
             x_codes = code_pool.tile([P, D_IN], U32, tag="x_codes", align_bytes=64)
             x_scales = code_pool.tile([P, D_IN], U8, tag="x_scales", align_bytes=64)
-            nc.vector.quantize_mx(
-                out=g_codes[:].bitcast(E5M2X4),
-                scales=g_scales[:],
-                in_=g_grp[:].rearrange("p w j -> p (w j)"),
-            )
-            nc.vector.quantize_mx(
-                out=x_codes[:].bitcast(E4M3X4),
-                scales=x_scales[:],
-                in_=x_grp[:].rearrange("p w j -> p (w j)"),
-            )
+            if c < LAST:
+                quantise(g_codes, g_scales, g_grp, 0, D_OUT, E5M2X4)
+            quantise(x_codes, x_scales, x_grp, 0, D_IN, E4M3X4)
             for m in range(M_TILES):
-                cols = slice(m * P, (m + 1) * P)
+                lo = m * P
+                hi = lo + P
+                if c == LAST:
+                    quantise(g_codes, g_scales, g_grp, lo, hi, E5M2X4)
                 nc.tensor.matmul_mx(
                     out=acc[m][:],
-                    lhsT=g_codes[:, cols].bitcast(E5M2X4),
-                    lhsT_scale=g_scales[:, cols],
+                    lhsT=g_codes[:, lo:hi].bitcast(E5M2X4),
+                    lhsT_scale=g_scales[:, lo:hi],
                     rhs=x_codes[:].bitcast(E4M3X4),
                     rhs_scale=x_scales[:],
                     start=(c == 0),
-                    stop=(c == PASSES - 1),
+                    stop=(c == LAST),
                 )
+            if c + 1 < LAST:
+                grouped = copies(c + 1, bank)
+            elif c + 1 == LAST:
+                grouped = last_copies()
 
         for m in range(M_TILES):
             res = res_pool.tile([P, D_IN], F32, tag="res")
             if m % 2 == 0:
-                nc.vector.tensor_copy(out=res[:], in_=acc[m][:])
-            else:
                 nc.scalar.copy(out=res[:], in_=acc[m][:])
+            else:
+                nc.vector.tensor_copy(out=res[:], in_=acc[m][:])
             nc.sync.dma_start(out=out[m * P : (m + 1) * P, :], in_=res[:])

@@ -1,7 +1,6 @@
 from contextlib import ExitStack
 
 import concourse.mybir as mybir
-from concourse.masks import make_identity
 
 F32 = mybir.dt.float32
 BF16 = mybir.dt.bfloat16
@@ -19,10 +18,7 @@ D_OUT = 512
 PASSES = TOKENS // K_PASS
 LAST = PASSES - 1
 M_TILES = D_OUT // P
-HALF = 256
 
-TENSOR_PASSES = range(7, 15)
-S_X_COLS = 112
 LAST_S_X_COLS = 320
 
 FLOPS = 2 * TOKENS * D_IN * D_OUT
@@ -43,13 +39,11 @@ def tile_quantlinearwrapper_t_kernel(tc, x, W, b, grad_out, out):
 
     with ExitStack() as ctx:
         ctx.enter_context(tc.manual_schedule())
-        const_pool = ctx.enter_context(tc.tile_pool(name="const", bufs=1))
         raw_pool = ctx.enter_context(tc.tile_pool(name="raw", bufs=PASSES))
         grp_pool = ctx.enter_context(tc.tile_pool(name="grp", bufs=3))
         code_pool = ctx.enter_context(tc.tile_pool(name="code", bufs=3))
         res_pool = ctx.enter_context(tc.tile_pool(name="res", bufs=M_TILES))
         psum = ctx.enter_context(tc.psum_pool(name="acc", bufs=1))
-        mv_psum = ctx.enter_context(tc.psum_pool(name="mv", bufs=2))
 
         g_raw = {}
         x_raw = {}
@@ -66,44 +60,17 @@ def tile_quantlinearwrapper_t_kernel(tc, x, W, b, grad_out, out):
         load(x_raw, x_rows, LAST, "x_raw")
         load(g_raw, g_rows, LAST, "g_raw")
 
-        ident = const_pool.tile([P, P], BF16)
-        make_identity(nc, ident[:])
-
         acc = [psum.tile([P, D_IN], F32, tag="acc%d" % m, name="acc%d" % m) for m in range(M_TILES)]
-
-        def tensor_part(c):
-            if c not in TENSOR_PASSES:
-                return None
-            bank = mv_psum.tile([P, HALF, PACK], BF16, tag="bank", name="bank")
-            for j in (1, 0, 3, 2):
-                cols = g_raw[c][:, j, 0:HALF]
-                if j % 2 == 1:
-                    nc.tensor.matmul(
-                        out=bank[:, :, j - 1 : j + 1],
-                        lhsT=ident[:],
-                        rhs=cols.unsqueeze(2).to_broadcast([P, HALF, 2]),
-                        start=True,
-                        stop=True,
-                    )
-                else:
-                    nc.tensor.matmul(out=bank[:, :, j], lhsT=ident[:], rhs=cols, start=True, stop=True)
-            return bank
 
         def new_tiles():
             g_grp = grp_pool.tile([P, D_OUT, PACK], BF16, tag="g_grp", align_bytes=64, name="g_grp")
             x_grp = grp_pool.tile([P, D_IN, PACK], BF16, tag="x_grp", align_bytes=64, name="x_grp")
             return g_grp, x_grp
 
-        def copies(c, bank):
+        def copies(c):
             g_grp, x_grp = new_tiles()
-            if bank is None:
-                regroup(nc.scalar.copy, g_grp, g_raw[c], 0, D_OUT)
-                regroup(nc.vector.tensor_copy, x_grp, x_raw[c], 0, D_IN)
-            else:
-                regroup(nc.scalar.copy, g_grp, g_raw[c], HALF, D_OUT)
-                nc.scalar.copy(out=g_grp[:, 0:HALF, :], in_=bank[:])
-                regroup(nc.scalar.copy, x_grp, x_raw[c], 0, S_X_COLS)
-                regroup(nc.vector.tensor_copy, x_grp, x_raw[c], S_X_COLS, D_IN)
+            regroup(nc.scalar.copy, g_grp, g_raw[c], 0, D_OUT)
+            regroup(nc.vector.tensor_copy, x_grp, x_raw[c], 0, D_IN)
             return g_grp, x_grp
 
         def last_copies():
@@ -122,10 +89,9 @@ def tile_quantlinearwrapper_t_kernel(tc, x, W, b, grad_out, out):
                 in_=grouped[:, lo:hi, :].rearrange("p w j -> p (w j)"),
             )
 
-        grouped = copies(0, tensor_part(0))
+        grouped = copies(0)
         for c in range(PASSES):
             g_grp, x_grp = grouped
-            bank = tensor_part(c + 1)
 
             g_codes = code_pool.tile([P, D_OUT], U32, tag="g_codes", align_bytes=64)
             g_scales = code_pool.tile([P, D_OUT], U8, tag="g_scales", align_bytes=64)
@@ -149,7 +115,7 @@ def tile_quantlinearwrapper_t_kernel(tc, x, W, b, grad_out, out):
                     stop=(c == LAST),
                 )
             if c + 1 < LAST:
-                grouped = copies(c + 1, bank)
+                grouped = copies(c + 1)
             elif c + 1 == LAST:
                 grouped = last_copies()
 

@@ -20,6 +20,7 @@ LAST = PASSES - 1
 M_TILES = D_OUT // P
 
 LAST_S_X_COLS = 320
+RUN = 8
 
 FLOPS = 2 * TOKENS * D_IN * D_OUT
 BYTES = 2 * TOKENS * (D_IN + D_OUT) + 4 * D_IN * D_OUT
@@ -27,8 +28,8 @@ BYTES = 2 * TOKENS * (D_IN + D_OUT) + 4 * D_IN * D_OUT
 
 def regroup(engine_copy, grouped, raw, lo, hi):
     engine_copy(
-        out=grouped[:, lo:hi, :].rearrange("p (c i) t -> p c t i", i=4),
-        in_=raw[:, :, lo:hi].rearrange("p t (c i) -> p c t i", i=4),
+        out=grouped[:, lo:hi, :].rearrange("p (c i) t -> p c t i", i=RUN),
+        in_=raw[:, :, lo:hi].rearrange("p t (c i) -> p c t i", i=RUN),
     )
 
 

@@ -90,40 +90,61 @@ def tile_quantlinearwrapper_t_kernel(tc, x, W, b, grad_out, out):
                 in_=grouped[:, lo:hi, :].rearrange("p w j -> p (w j)"),
             )
 
+        def code_tiles():
+            g_codes = code_pool.tile([P, D_OUT], U32, tag="g_codes", align_bytes=64, name="g_codes")
+            g_scales = code_pool.tile([P, D_OUT], U8, tag="g_scales", align_bytes=64, name="g_scales")
+            x_codes = code_pool.tile([P, D_IN], U32, tag="x_codes", align_bytes=64, name="x_codes")
+            x_scales = code_pool.tile([P, D_IN], U8, tag="x_scales", align_bytes=64, name="x_scales")
+            return g_codes, g_scales, x_codes, x_scales
+
+        def multiply(c, m, tiles):
+            g_codes, g_scales, x_codes, x_scales = tiles
+            lo = m * P
+            nc.tensor.matmul_mx(
+                out=acc[m][:],
+                lhsT=g_codes[:, lo : lo + P].bitcast(E5M2X4),
+                lhsT_scale=g_scales[:, lo : lo + P],
+                rhs=x_codes[:].bitcast(E4M3X4),
+                rhs_scale=x_scales[:],
+                start=(c == 0),
+                stop=(c == LAST),
+            )
+
+        def quantise_g(tiles, g_grp, lo, hi):
+            quantise(tiles[0], tiles[1], g_grp, lo, hi, E5M2X4)
+
+        def quantise_x(tiles, x_grp):
+            quantise(tiles[2], tiles[3], x_grp, 0, D_IN, E4M3X4)
+
         grouped = copies(0)
-        for c in range(PASSES):
+        for c in range(LAST - 1):
             g_grp, x_grp = grouped
-
-            g_codes = code_pool.tile([P, D_OUT], U32, tag="g_codes", align_bytes=64)
-            g_scales = code_pool.tile([P, D_OUT], U8, tag="g_scales", align_bytes=64)
-            x_codes = code_pool.tile([P, D_IN], U32, tag="x_codes", align_bytes=64)
-            x_scales = code_pool.tile([P, D_IN], U8, tag="x_scales", align_bytes=64)
-            if c < LAST:
-                quantise(g_codes, g_scales, g_grp, 0, D_OUT, E5M2X4)
-            quantise(x_codes, x_scales, x_grp, 0, D_IN, E4M3X4)
+            tiles = code_tiles()
+            quantise_g(tiles, g_grp, 0, D_OUT)
+            quantise_x(tiles, x_grp)
             for m in range(M_TILES):
-                lo = m * P
-                hi = lo + P
-                if c == LAST:
-                    quantise(g_codes, g_scales, g_grp, lo, hi, E5M2X4)
-                nc.tensor.matmul_mx(
-                    out=acc[m][:],
-                    lhsT=g_codes[:, lo:hi].bitcast(E5M2X4),
-                    lhsT_scale=g_scales[:, lo:hi],
-                    rhs=x_codes[:].bitcast(E4M3X4),
-                    rhs_scale=x_scales[:],
-                    start=(c == 0),
-                    stop=(c == LAST),
-                )
-            if c + 1 < LAST:
-                grouped = copies(c + 1)
-            elif c + 1 == LAST:
-                grouped = last_copies()
+                multiply(c, m, tiles)
+            grouped = copies(c + 1)
 
+        g_prev, x_prev = grouped
+        prev = code_tiles()
+        quantise_g(prev, g_prev, 0, P)
+        quantise_x(prev, x_prev)
+        multiply(LAST - 1, 0, prev)
+        g_grp, x_grp = last_copies()
+        tiles = code_tiles()
+        quantise_x(tiles, x_grp)
         for m in range(M_TILES):
-            res = res_pool.tile([P, D_IN], F32, tag="res")
-            if m % 2 == 0:
+            lo = m * P
+            hi = lo + P
+            if m > 0:
+                quantise_g(prev, g_prev, lo, hi)
+                multiply(LAST - 1, m, prev)
+            quantise_g(tiles, g_grp, lo, hi)
+            multiply(LAST, m, tiles)
+            res = res_pool.tile([P, D_IN], F32, tag="res", name="res")
+            if m < M_TILES - 1:
                 nc.scalar.copy(out=res[:], in_=acc[m][:])
             else:
                 nc.vector.tensor_copy(out=res[:], in_=acc[m][:])
-            nc.sync.dma_start(out=out[m * P : (m + 1) * P, :], in_=res[:])
+            nc.sync.dma_start(out=out[lo:hi, :], in_=res[:])

from contextlib import ExitStack

import concourse.mybir as mybir

F32 = mybir.dt.float32
BF16 = mybir.dt.bfloat16
U32 = mybir.dt.uint32
U8 = mybir.dt.uint8
E4M3X4 = mybir.dt.float8_e4m3fn_x4
E5M2X4 = mybir.dt.float8_e5m2_x4

P = 128
PACK = 4
K_PASS = P * PACK
TOKENS = 8192
D_IN = 512
D_OUT = 512
PASSES = TOKENS // K_PASS
LAST = PASSES - 1
M_TILES = D_OUT // P

LAST_S_X_COLS = 320
RUN = 8

FLOPS = 2 * TOKENS * D_IN * D_OUT
BYTES = 2 * TOKENS * (D_IN + D_OUT) + 4 * D_IN * D_OUT


def regroup(engine_copy, grouped, raw, lo, hi):
    engine_copy(
        out=grouped[:, lo:hi, :].rearrange("p (c i) t -> p c t i", i=RUN),
        in_=raw[:, :, lo:hi].rearrange("p t (c i) -> p c t i", i=RUN),
    )


def tile_quantlinearwrapper_t_kernel(tc, x, W, b, grad_out, out):
    nc = tc.nc
    x_rows = x.flatten_outer_dims()
    g_rows = grad_out.flatten_outer_dims()

    with ExitStack() as ctx:
        ctx.enter_context(tc.manual_schedule())
        raw_pool = ctx.enter_context(tc.tile_pool(name="raw", bufs=PASSES))
        grp_pool = ctx.enter_context(tc.tile_pool(name="grp", bufs=3))
        code_pool = ctx.enter_context(tc.tile_pool(name="code", bufs=3))
        res_pool = ctx.enter_context(tc.tile_pool(name="res", bufs=M_TILES))
        psum = ctx.enter_context(tc.psum_pool(name="acc", bufs=1))

        g_raw = {}
        x_raw = {}

        def load(store, rows_ap, c, tag):
            rows = slice(c * K_PASS, (c + 1) * K_PASS)
            raw = raw_pool.tile([P, PACK, D_IN], BF16, tag=tag, name=tag)
            nc.sync.dma_start(out=raw[:], in_=rows_ap[rows, :].rearrange("(p j) w -> p j w", j=PACK))
            store[c] = raw

        for c in range(LAST):
            load(g_raw, g_rows, c, "g_raw")
            load(x_raw, x_rows, c, "x_raw")
        load(x_raw, x_rows, LAST, "x_raw")
        load(g_raw, g_rows, LAST, "g_raw")

        acc = [psum.tile([P, D_IN], F32, tag="acc%d" % m, name="acc%d" % m) for m in range(M_TILES)]

        def new_tiles():
            g_grp = grp_pool.tile([P, D_OUT, PACK], BF16, tag="g_grp", align_bytes=64, name="g_grp")
            x_grp = grp_pool.tile([P, D_IN, PACK], BF16, tag="x_grp", align_bytes=64, name="x_grp")
            return g_grp, x_grp

        def copies(c):
            g_grp, x_grp = new_tiles()
            regroup(nc.scalar.copy, g_grp, g_raw[c], 0, D_OUT)
            regroup(nc.vector.tensor_copy, x_grp, x_raw[c], 0, D_IN)
            return g_grp, x_grp

        def last_copies():
            g_grp, x_grp = new_tiles()
            regroup(nc.scalar.copy, x_grp, x_raw[LAST], 0, LAST_S_X_COLS)
            regroup(nc.vector.tensor_copy, x_grp, x_raw[LAST], LAST_S_X_COLS, D_IN)
            regroup(nc.vector.tensor_copy, g_grp, g_raw[LAST], 0, P)
            for m in range(1, M_TILES):
                regroup(nc.scalar.copy, g_grp, g_raw[LAST], m * P, (m + 1) * P)
            return g_grp, x_grp

        def quantise(codes, scales, grouped, lo, hi, fmt):
            nc.vector.quantize_mx(
                out=codes[:, lo:hi].bitcast(fmt),
                scales=scales[:, lo:hi],
                in_=grouped[:, lo:hi, :].rearrange("p w j -> p (w j)"),
            )

        def code_tiles():
            g_codes = code_pool.tile([P, D_OUT], U32, tag="g_codes", align_bytes=64, name="g_codes")
            g_scales = code_pool.tile([P, D_OUT], U8, tag="g_scales", align_bytes=64, name="g_scales")
            x_codes = code_pool.tile([P, D_IN], U32, tag="x_codes", align_bytes=64, name="x_codes")
            x_scales = code_pool.tile([P, D_IN], U8, tag="x_scales", align_bytes=64, name="x_scales")
            return g_codes, g_scales, x_codes, x_scales

        def multiply(c, m, tiles):
            g_codes, g_scales, x_codes, x_scales = tiles
            lo = m * P
            nc.tensor.matmul_mx(
                out=acc[m][:],
                lhsT=g_codes[:, lo : lo + P].bitcast(E5M2X4),
                lhsT_scale=g_scales[:, lo : lo + P],
                rhs=x_codes[:].bitcast(E4M3X4),
                rhs_scale=x_scales[:],
                start=(c == 0),
                stop=(c == LAST),
            )

        def quantise_g(tiles, g_grp, lo, hi):
            quantise(tiles[0], tiles[1], g_grp, lo, hi, E5M2X4)

        def quantise_x(tiles, x_grp):
            quantise(tiles[2], tiles[3], x_grp, 0, D_IN, E4M3X4)

        grouped = copies(0)
        for c in range(LAST - 1):
            g_grp, x_grp = grouped
            tiles = code_tiles()
            quantise_g(tiles, g_grp, 0, D_OUT)
            quantise_x(tiles, x_grp)
            for m in range(M_TILES):
                multiply(c, m, tiles)
            grouped = copies(c + 1)

        g_prev, x_prev = grouped
        prev = code_tiles()
        quantise_g(prev, g_prev, 0, P)
        quantise_x(prev, x_prev)
        multiply(LAST - 1, 0, prev)
        g_grp, x_grp = last_copies()
        tiles = code_tiles()
        quantise_x(tiles, x_grp)
        for m in range(M_TILES):
            lo = m * P
            hi = lo + P
            if m > 0:
                quantise_g(prev, g_prev, lo, hi)
                multiply(LAST - 1, m, prev)
            quantise_g(tiles, g_grp, lo, hi)
            multiply(LAST, m, tiles)
            res = res_pool.tile([P, D_IN], F32, tag="res", name="res")
            if m < M_TILES - 1:
                nc.scalar.copy(out=res[:], in_=acc[m][:])
            else:
                nc.vector.tensor_copy(out=res[:], in_=acc[m][:])
            nc.sync.dma_start(out=out[lo:hi, :], in_=res[:])
